import numpy as np
import ml_dtypes


def mxq(x, axis, fmt="e4m3"):
    dtype, down = {"e4m3": (ml_dtypes.float8_e4m3fn, 7), "e5m2": (ml_dtypes.float8_e5m2, 14)}[fmt]
    v = np.moveaxis(np.asarray(x, np.float32).astype(ml_dtypes.bfloat16).astype(np.float64), axis, -1)
    blocks = v.reshape(v.shape[:-1] + (-1, 32))
    amax = np.abs(blocks).max(-1, keepdims=True)
    byte = np.maximum(np.where(amax > 0, np.frexp(amax)[1] - 1 + 127, 0) - down, 1)
    scale = np.exp2(byte - 127.0)
    codes = (blocks / scale).astype(np.float32).astype(dtype).astype(np.float64)
    return np.moveaxis((codes * scale).reshape(v.shape), -1, axis)


WIDE = False


def mx_kscale(k):
    if not WIDE:
        return np.ones(k)
    levels = np.array([10, -10, 5, -5, 0])
    a = np.random.permutation(np.resize(levels, k // 512 * 4)).reshape(k // 512, 4)
    idx = np.arange(k)
    return np.exp2(a[idx // 512, idx % 128 // 32])


BF16 = ml_dtypes.bfloat16


def bf(x):
    return np.asarray(x, np.float32).astype(BF16)


def f64(x):
    return np.asarray(x).astype(np.float64)


B, F, O = 1024, 2048, 1024


def setup_inputs():
    s = mx_kscale(F)
    return {"x": bf(np.random.standard_normal((B, 2, F)) * s),
            "filters_real": bf(np.random.standard_normal((O, F)) * 0.5 / np.sqrt(F) / s),
            "filters_imag": bf(np.random.standard_normal((O, F)) * 0.5 / np.sqrt(F) / s)}


def reference(x, filters_real, filters_imag):
    x = f64(x)
    x_real = x[:, 0]
    x_imag = x[:, 1]
    w_r = f64(filters_real) + f64(filters_imag)
    w_i = f64(filters_real) - f64(filters_imag)
    energies = (mxq(x_real, 1, "e4m3") @ mxq(w_r, 1, "e4m3").T) + (mxq(x_imag, 1, "e4m3") @ mxq(w_i, 1, "e4m3").T)
    return energies

@@ -1,0 +1,147 @@
+from contextlib import ExitStack
+
+import concourse.mybir as mybir
+from concourse.masks import make_identity
+
+F32 = mybir.dt.float32
+BF16 = mybir.dt.bfloat16
+U32 = mybir.dt.uint32
+U8 = mybir.dt.uint8
+FP8X4 = mybir.dt.float8_e4m3fn_x4
+ADD = mybir.AluOpType.add
+SUB = mybir.AluOpType.subtract
+
+P = 128
+B, F, O = 1024, 2048, 1024
+FLOPS = 2 * B * O * 2 * F
+PASSES = 8
+NCOL = 256
+
+UNITS = (
+    ("W", 0), ("W", 1), ("X", 0), ("X", 1), ("X", 2), ("X", 3), ("W", 2), ("W", 3),
+    ("X", 4), ("X", 5), ("X", 6), ("X", 7), ("W", 4), ("W", 5), ("W", 6), ("W", 7),
+)
+LAG_W = 3
+LAG_X = 3
+RAW_BUFS = 6
+STAGE_BUFS = 8
+
+
+def pe_sequence():
+    pos = {}
+    for n, u in enumerate(UNITS):
+        pos[u] = n
+    items = []
+    for j in range(O // NCOL):
+        for i in range(B // P):
+            avail = max(pos[("X", i)] + LAG_X, pos[("W", 2 * j)] + LAG_W, pos[("W", 2 * j + 1)] + LAG_W)
+            items.append((avail, j, i))
+    items = sorted(items)
+    seq = []
+    for n in range(len(UNITS)):
+        seq.append(("T", n, 0))
+        if items and items[0][0] <= n:
+            seq.append(("M", items[0][2], items[0][1]))
+            items = items[1:]
+    for it in items:
+        seq.append(("M", it[2], it[1]))
+    return seq
+
+
+def tile_fftmlp_kernel(tc, x, filters_real, filters_imag, out):
+    nc = tc.nc
+    with ExitStack() as ctx:
+        keep = ctx.enter_context(tc.tile_pool(name="keep", bufs=1))
+        raw_pool = ctx.enter_context(tc.tile_pool(name="rawp", bufs=RAW_BUFS))
+        stage_pool = ctx.enter_context(tc.tile_pool(name="stagep", bufs=STAGE_BUFS))
+        wg_pool = ctx.enter_context(tc.tile_pool(name="wgp", bufs=2))
+        res_pool = ctx.enter_context(tc.tile_pool(name="resp", bufs=4))
+        tp_pool = ctx.enter_context(tc.psum_pool(name="tpp", bufs=4))
+        acc_pool = ctx.enter_context(tc.psum_pool(name="accp", bufs=4))
+        ctx.enter_context(tc.manual_schedule())
+
+        ident = keep.tile([P, P], F32, name="ident")
+        make_identity(nc, ident[:])
+
+        x_codes = [keep.tile([P, PASSES * P], U32, name="xc%d" % i, align_bytes=64) for i in range(B // P)]
+        x_scales = [keep.tile([P, PASSES * P], U8, name="xs%d" % i, align_bytes=64) for i in range(B // P)]
+        w_codes = [keep.tile([P, PASSES, NCOL], U32, name="wc%d" % j, align_bytes=64) for j in range(O // NCOL)]
+        w_scales = [keep.tile([P, PASSES, NCOL], U8, name="ws%d" % j, align_bytes=64) for j in range(O // NCOL)]
+
+        raws = {}
+
+        def load(n):
+            kind, idx = UNITS[n]
+            raw = raw_pool.tile([P, 2 * F], BF16, name="raw", tag="raw")
+            rows = slice(idx * P, (idx + 1) * P)
+            if kind == "X":
+                nc.sync.dma_start(out=raw[:], in_=x[rows, :, :].rearrange("m c k -> m (c k)"))
+            else:
+                cuts = 2 if n == 0 else 1
+                step = F // cuts
+                for h in range(cuts):
+                    cols = slice(h * step, (h + 1) * step)
+                    nc.sync.dma_start(out=raw[:, h * step:(h + 1) * step], in_=filters_real[rows, cols])
+                    nc.sync.dma_start(out=raw[:, F + h * step:F + (h + 1) * step], in_=filters_imag[rows, cols])
+            raws[n] = raw
+
+        def transpose_unit(n):
+            kind, idx = UNITS[n]
+            words = raws[n][:].bitcast(F32)
+            stage = stage_pool.tile([P, 2 * F], BF16, name="stage", tag="stage", align_bytes=64)
+            stage_words = stage[:].bitcast(F32)
+            for b in range(4):
+                tp = tp_pool.tile([P, 512], F32, name="tp", tag="tp")
+                if kind == "X":
+                    blocks = [4 * b, 4 * b + 1, 4 * b + 2, 4 * b + 3]
+                else:
+                    blocks = [2 * b, 2 * b + 1, 8 + 2 * b, 8 + 2 * b + 1]
+                for s in range(4):
+                    nc.tensor.transpose(tp[:, s * P:(s + 1) * P], words[:, blocks[s] * P:(blocks[s] + 1) * P], ident[:])
+                src = tp[:].rearrange("p (g u m) -> p g m u", g=2, u=2)
+                if kind == "X":
+                    dst = stage_words[:, b * 512:(b + 1) * 512].rearrange("p (g m u) -> p g m u", g=2, u=2)
+                else:
+                    dst = stage_words.rearrange("p (f c m u) -> p f c m u", f=2, c=4, u=2)[:, :, b, :, :]
+                nc.scalar.copy(out=dst, in_=src)
+            if kind == "X":
+                nc.vector.quantize_mx(out=x_codes[idx][:].bitcast(FP8X4), scales=x_scales[idx][:], in_=stage[:])
+            else:
+                wg = wg_pool.tile([P, 2 * F], BF16, name="wg", tag="wg", align_bytes=64)
+                nc.vector.tensor_tensor(out=wg[:, 0:F], in0=stage[:, 0:F], in1=stage[:, F:2 * F], op=ADD)
+                nc.vector.tensor_tensor(out=wg[:, F:2 * F], in0=stage[:, 0:F], in1=stage[:, F:2 * F], op=SUB)
+                cols = slice((idx % 2) * P, (idx % 2 + 1) * P)
+                for g in range(PASSES):
+                    nc.vector.quantize_mx(
+                        out=w_codes[idx // 2][:, g, cols].bitcast(FP8X4),
+                        scales=w_scales[idx // 2][:, g, cols],
+                        in_=wg[:, g * 512:(g + 1) * 512],
+                    )
+
+        def multiply(i, j):
+            acc = acc_pool.tile([P, NCOL], F32, name="acc", tag="acc")
+            for g in range(PASSES):
+                nc.tensor.matmul_mx(
+                    out=acc[:],
+                    lhsT=x_codes[i][:, g * P:(g + 1) * P].bitcast(FP8X4),
+                    lhsT_scale=x_scales[i][:, g * P:(g + 1) * P],
+                    rhs=w_codes[j][:, g, :].bitcast(FP8X4),
+                    rhs_scale=w_scales[j][:, g, :],
+                    start=(g == 0),
+                    stop=(g == PASSES - 1),
+                )
+            res = res_pool.tile([P, NCOL], F32, name="res", tag="res")
+            nc.scalar.copy(out=res[:], in_=acc[:])
+            nc.sync.dma_start(out=out[i * P:(i + 1) * P, j * NCOL:(j + 1) * NCOL], in_=res[:])
+
+        for n in range(RAW_BUFS):
+            load(n)
+        loaded = RAW_BUFS
+        for step in pe_sequence():
+            if step[0] == "T":
+                transpose_unit(step[1])
+                if loaded < len(UNITS):
+                    load(loaded)
+                    loaded += 1
+            else:
+                multiply(step[1], step[2])

@@ -15,16 +15,23 @@ P = 128
 B, F, O = 1024, 2048, 1024
 FLOPS = 2 * B * O * 2 * F
 PASSES = 8
-NCOL = 256
+PAIR = 2 * P
 
 UNITS = (
-    ("W", 0), ("W", 1), ("X", 0), ("X", 1), ("X", 2), ("X", 3), ("W", 2), ("W", 3),
-    ("X", 4), ("X", 5), ("X", 6), ("X", 7), ("W", 4), ("W", 5), ("W", 6), ("W", 7),
+    ("W", 0), ("X", 0), ("X", 1), ("X", 2), ("W", 1), ("X", 3), ("X", 4), ("W", 2),
+    ("X", 5), ("W", 3), ("X", 6), ("X", 7), ("W", 4), ("W", 5), ("W", 6), ("W", 7),
 )
-LAG_W = 3
-LAG_X = 3
+LAG_W = 2
+LAG_X = 2
+GROUPS_PER_UNIT = 2
 RAW_BUFS = 6
 STAGE_BUFS = 8
+TP_BANKS = 5
+ACC_BANKS = 3
+WARM_FIRST = 6
+WARM_EACH = 2
+WARM_UNITS = 3
+SPLIT_LOADS = 4
 
 
 def pe_sequence():
@@ -32,19 +39,27 @@ def pe_sequence():
     for n, u in enumerate(UNITS):
         pos[u] = n
     items = []
-    for j in range(O // NCOL):
-        for i in range(B // P):
-            avail = max(pos[("X", i)] + LAG_X, pos[("W", 2 * j)] + LAG_W, pos[("W", 2 * j + 1)] + LAG_W)
-            items.append((avail, j, i))
+    for i in range(B // P):
+        for j in range(O // PAIR):
+            a, b = pos[("W", 2 * j)], pos[("W", 2 * j + 1)]
+            if abs(a - b) > 1 and pos[("X", i)] < max(a, b):
+                parts = [(2 * j,), (2 * j + 1,)]
+            else:
+                parts = [(2 * j, 2 * j + 1)]
+            for ws in parts:
+                avail = max([pos[("X", i)] + LAG_X] + [pos[("W", w)] + LAG_W for w in ws])
+                items.append((avail, ws[0], i, ws))
     items = sorted(items)
     seq = []
     for n in range(len(UNITS)):
-        seq.append(("T", n, 0))
-        if items and items[0][0] <= n:
-            seq.append(("M", items[0][2], items[0][1]))
+        seq.append(("T", n, ()))
+        budget = 2 * GROUPS_PER_UNIT
+        while budget > 0 and items and items[0][0] <= n:
+            seq.append(("M", items[0][2], items[0][3]))
+            budget -= len(items[0][3])
             items = items[1:]
     for it in items:
-        seq.append(("M", it[2], it[1]))
+        seq.append(("M", it[2], it[3]))
     return seq
 
 
@@ -56,17 +71,19 @@ def tile_fftmlp_kernel(tc, x, filters_real, filters_imag, out):
         stage_pool = ctx.enter_context(tc.tile_pool(name="stagep", bufs=STAGE_BUFS))
         wg_pool = ctx.enter_context(tc.tile_pool(name="wgp", bufs=2))
         res_pool = ctx.enter_context(tc.tile_pool(name="resp", bufs=4))
-        tp_pool = ctx.enter_context(tc.psum_pool(name="tpp", bufs=4))
-        acc_pool = ctx.enter_context(tc.psum_pool(name="accp", bufs=4))
+        tp_pool = ctx.enter_context(tc.psum_pool(name="tpp", bufs=TP_BANKS))
+        acc_pool = ctx.enter_context(tc.psum_pool(name="accp", bufs=ACC_BANKS))
         ctx.enter_context(tc.manual_schedule())
 
+        warm = keep.tile([P, 512], BF16, name="warm")
+        nc.vector.memset(warm[:], 0.0)
         ident = keep.tile([P, P], F32, name="ident")
         make_identity(nc, ident[:])
 
         x_codes = [keep.tile([P, PASSES * P], U32, name="xc%d" % i, align_bytes=64) for i in range(B // P)]
         x_scales = [keep.tile([P, PASSES * P], U8, name="xs%d" % i, align_bytes=64) for i in range(B // P)]
-        w_codes = [keep.tile([P, PASSES, NCOL], U32, name="wc%d" % j, align_bytes=64) for j in range(O // NCOL)]
-        w_scales = [keep.tile([P, PASSES, NCOL], U8, name="ws%d" % j, align_bytes=64) for j in range(O // NCOL)]
+        w_codes = [keep.tile([P, PASSES, PAIR], U32, name="wc%d" % j, align_bytes=64) for j in range(O // PAIR)]
+        w_scales = [keep.tile([P, PASSES, PAIR], U8, name="ws%d" % j, align_bytes=64) for j in range(O // PAIR)]
 
         raws = {}
 
@@ -75,9 +92,13 @@ def tile_fftmlp_kernel(tc, x, filters_real, filters_imag, out):
             raw = raw_pool.tile([P, 2 * F], BF16, name="raw", tag="raw")
             rows = slice(idx * P, (idx + 1) * P)
             if kind == "X":
-                nc.sync.dma_start(out=raw[:], in_=x[rows, :, :].rearrange("m c k -> m (c k)"))
+                if n < SPLIT_LOADS:
+                    nc.sync.dma_start(out=raw[:, 0:F], in_=x[rows, 0, :])
+                    nc.sync.dma_start(out=raw[:, F:2 * F], in_=x[rows, 1, :])
+                else:
+                    nc.sync.dma_start(out=raw[:], in_=x[rows, :, :].rearrange("m c k -> m (c k)"))
             else:
-                cuts = 2 if n == 0 else 1
+                cuts = 2 if n < SPLIT_LOADS else 1
                 step = F // cuts
                 for h in range(cuts):
                     cols = slice(h * step, (h + 1) * step)
@@ -85,11 +106,20 @@ def tile_fftmlp_kernel(tc, x, filters_real, filters_imag, out):
                     nc.sync.dma_start(out=raw[:, F + h * step:F + (h + 1) * step], in_=filters_imag[rows, cols])
             raws[n] = raw
 
+        warm_ps = acc_pool.tile([P, 512], F32, name="warm_ps", tag="acc")
+
+        def warm_up(count):
+            for d in range(count):
+                nc.tensor.matmul(out=warm_ps[:], lhsT=warm[:, 0:P], rhs=warm[:], start=True, stop=True)
+
         def transpose_unit(n):
             kind, idx = UNITS[n]
             words = raws[n][:].bitcast(F32)
             stage = stage_pool.tile([P, 2 * F], BF16, name="stage", tag="stage", align_bytes=64)
             stage_words = stage[:].bitcast(F32)
+            wg = None
+            if kind == "W":
+                wg = wg_pool.tile([P, 2 * F], BF16, name="wg", tag="wg", align_bytes=64)
             for b in range(4):
                 tp = tp_pool.tile([P, 512], F32, name="tp", tag="tp")
                 if kind == "X":
@@ -103,43 +133,59 @@ def tile_fftmlp_kernel(tc, x, filters_real, filters_imag, out):
                     dst = stage_words[:, b * 512:(b + 1) * 512].rearrange("p (g m u) -> p g m u", g=2, u=2)
                 else:
                     dst = stage_words.rearrange("p (f c m u) -> p f c m u", f=2, c=4, u=2)[:, :, b, :, :]
-                nc.scalar.copy(out=dst, in_=src)
-            if kind == "X":
-                nc.vector.quantize_mx(out=x_codes[idx][:].bitcast(FP8X4), scales=x_scales[idx][:], in_=stage[:])
-            else:
-                wg = wg_pool.tile([P, 2 * F], BF16, name="wg", tag="wg", align_bytes=64)
-                nc.vector.tensor_tensor(out=wg[:, 0:F], in0=stage[:, 0:F], in1=stage[:, F:2 * F], op=ADD)
-                nc.vector.tensor_tensor(out=wg[:, F:2 * F], in0=stage[:, 0:F], in1=stage[:, F:2 * F], op=SUB)
-                cols = slice((idx % 2) * P, (idx % 2 + 1) * P)
-                for g in range(PASSES):
+                if kind == "X" and b == 3:
+                    nc.vector.tensor_copy(out=dst, in_=src)
+                else:
+                    nc.scalar.copy(out=dst, in_=src)
+                if b % 2 == 0:
+                    continue
+                h = b // 2
+                if kind == "X":
                     nc.vector.quantize_mx(
-                        out=w_codes[idx // 2][:, g, cols].bitcast(FP8X4),
-                        scales=w_scales[idx // 2][:, g, cols],
-                        in_=wg[:, g * 512:(g + 1) * 512],
+                        out=x_codes[idx][:, h * 512:(h + 1) * 512].bitcast(FP8X4),
+                        scales=x_scales[idx][:, h * 512:(h + 1) * 512],
+                        in_=stage[:, h * F:(h + 1) * F],
                     )
+                else:
+                    lo, hi = h * 1024, (h + 1) * 1024
+                    nc.vector.tensor_tensor(out=wg[:, lo:hi], in0=stage[:, lo:hi], in1=stage[:, F + lo:F + hi], op=ADD)
+                    nc.vector.tensor_tensor(out=wg[:, F + lo:F + hi], in0=stage[:, lo:hi], in1=stage[:, F + lo:F + hi], op=SUB)
+                    cols = slice((idx % 2) * P, (idx % 2 + 1) * P)
+                    for g in (2 * h, 2 * h + 1, 4 + 2 * h, 4 + 2 * h + 1):
+                        nc.vector.quantize_mx(
+                            out=w_codes[idx // 2][:, g, cols].bitcast(FP8X4),
+                            scales=w_scales[idx // 2][:, g, cols],
+                            in_=wg[:, g * 512:(g + 1) * 512],
+                        )
 
-        def multiply(i, j):
-            acc = acc_pool.tile([P, NCOL], F32, name="acc", tag="acc")
+        def multiply(i, ws):
+            width = len(ws) * P
+            j = ws[0] // 2
+            cols = slice((ws[0] % 2) * P, (ws[0] % 2) * P + width)
+            acc = acc_pool.tile([P, 512], F32, name="acc", tag="acc")
             for g in range(PASSES):
                 nc.tensor.matmul_mx(
-                    out=acc[:],
+                    out=acc[:, 0:width],
                     lhsT=x_codes[i][:, g * P:(g + 1) * P].bitcast(FP8X4),
                     lhsT_scale=x_scales[i][:, g * P:(g + 1) * P],
-                    rhs=w_codes[j][:, g, :].bitcast(FP8X4),
-                    rhs_scale=w_scales[j][:, g, :],
+                    rhs=w_codes[j][:, g, cols].bitcast(FP8X4),
+                    rhs_scale=w_scales[j][:, g, cols],
                     start=(g == 0),
                     stop=(g == PASSES - 1),
                 )
-            res = res_pool.tile([P, NCOL], F32, name="res", tag="res")
-            nc.scalar.copy(out=res[:], in_=acc[:])
-            nc.sync.dma_start(out=out[i * P:(i + 1) * P, j * NCOL:(j + 1) * NCOL], in_=res[:])
+            res = res_pool.tile([P, PAIR], F32, name="res", tag="res")
+            nc.scalar.copy(out=res[:, 0:width], in_=acc[:, 0:width])
+            nc.sync.dma_start(out=out[i * P:(i + 1) * P, ws[0] * P:ws[0] * P + width], in_=res[:, 0:width])
 
         for n in range(RAW_BUFS):
             load(n)
         loaded = RAW_BUFS
+        warm_up(WARM_FIRST)
         for step in pe_sequence():
             if step[0] == "T":
                 transpose_unit(step[1])
+                if step[1] < WARM_UNITS:
+                    warm_up(WARM_EACH)
                 if loaded < len(UNITS):
                     load(loaded)
                     loaded += 1

@@ -15,23 +15,19 @@ P = 128
 B, F, O = 1024, 2048, 1024
 FLOPS = 2 * B * O * 2 * F
 PASSES = 8
-PAIR = 2 * P
+NCOL = 256
 
 UNITS = (
-    ("W", 0), ("X", 0), ("X", 1), ("X", 2), ("W", 1), ("X", 3), ("X", 4), ("W", 2),
-    ("X", 5), ("W", 3), ("X", 6), ("X", 7), ("W", 4), ("W", 5), ("W", 6), ("W", 7),
+    ("W", 0), ("W", 1), ("X", 0), ("X", 1), ("X", 2), ("X", 3), ("W", 2), ("W", 3),
+    ("X", 4), ("X", 5), ("X", 6), ("X", 7), ("W", 4), ("W", 5), ("W", 6), ("W", 7),
 )
-LAG_W = 2
-LAG_X = 2
-GROUPS_PER_UNIT = 2
+LAG_W = 3
+LAG_X = 3
 RAW_BUFS = 6
 STAGE_BUFS = 8
-TP_BANKS = 5
-ACC_BANKS = 3
 WARM_FIRST = 6
 WARM_EACH = 2
-WARM_UNITS = 3
-SPLIT_LOADS = 4
+WARM_UNITS = 6
 
 
 def pe_sequence():
@@ -39,27 +35,19 @@ def pe_sequence():
     for n, u in enumerate(UNITS):
         pos[u] = n
     items = []
-    for i in range(B // P):
-        for j in range(O // PAIR):
-            a, b = pos[("W", 2 * j)], pos[("W", 2 * j + 1)]
-            if abs(a - b) > 1 and pos[("X", i)] < max(a, b):
-                parts = [(2 * j,), (2 * j + 1,)]
-            else:
-                parts = [(2 * j, 2 * j + 1)]
-            for ws in parts:
-                avail = max([pos[("X", i)] + LAG_X] + [pos[("W", w)] + LAG_W for w in ws])
-                items.append((avail, ws[0], i, ws))
+    for j in range(O // NCOL):
+        for i in range(B // P):
+            avail = max(pos[("X", i)] + LAG_X, pos[("W", 2 * j)] + LAG_W, pos[("W", 2 * j + 1)] + LAG_W)
+            items.append((avail, j, i))
     items = sorted(items)
     seq = []
     for n in range(len(UNITS)):
-        seq.append(("T", n, ()))
-        budget = 2 * GROUPS_PER_UNIT
-        while budget > 0 and items and items[0][0] <= n:
-            seq.append(("M", items[0][2], items[0][3]))
-            budget -= len(items[0][3])
+        seq.append(("T", n, 0))
+        if items and items[0][0] <= n:
+            seq.append(("M", items[0][2], items[0][1]))
             items = items[1:]
     for it in items:
-        seq.append(("M", it[2], it[3]))
+        seq.append(("M", it[2], it[1]))
     return seq
 
 
@@ -71,8 +59,8 @@ def tile_fftmlp_kernel(tc, x, filters_real, filters_imag, out):
         stage_pool = ctx.enter_context(tc.tile_pool(name="stagep", bufs=STAGE_BUFS))
         wg_pool = ctx.enter_context(tc.tile_pool(name="wgp", bufs=2))
         res_pool = ctx.enter_context(tc.tile_pool(name="resp", bufs=4))
-        tp_pool = ctx.enter_context(tc.psum_pool(name="tpp", bufs=TP_BANKS))
-        acc_pool = ctx.enter_context(tc.psum_pool(name="accp", bufs=ACC_BANKS))
+        tp_pool = ctx.enter_context(tc.psum_pool(name="tpp", bufs=4))
+        acc_pool = ctx.enter_context(tc.psum_pool(name="accp", bufs=4))
         ctx.enter_context(tc.manual_schedule())
 
         warm = keep.tile([P, 512], BF16, name="warm")
@@ -82,8 +70,8 @@ def tile_fftmlp_kernel(tc, x, filters_real, filters_imag, out):
 
         x_codes = [keep.tile([P, PASSES * P], U32, name="xc%d" % i, align_bytes=64) for i in range(B // P)]
         x_scales = [keep.tile([P, PASSES * P], U8, name="xs%d" % i, align_bytes=64) for i in range(B // P)]
-        w_codes = [keep.tile([P, PASSES, PAIR], U32, name="wc%d" % j, align_bytes=64) for j in range(O // PAIR)]
-        w_scales = [keep.tile([P, PASSES, PAIR], U8, name="ws%d" % j, align_bytes=64) for j in range(O // PAIR)]
+        w_codes = [keep.tile([P, PASSES, NCOL], U32, name="wc%d" % j, align_bytes=64) for j in range(O // NCOL)]
+        w_scales = [keep.tile([P, PASSES, NCOL], U8, name="ws%d" % j, align_bytes=64) for j in range(O // NCOL)]
 
         raws = {}
 
@@ -92,13 +80,9 @@ def tile_fftmlp_kernel(tc, x, filters_real, filters_imag, out):
             raw = raw_pool.tile([P, 2 * F], BF16, name="raw", tag="raw")
             rows = slice(idx * P, (idx + 1) * P)
             if kind == "X":
-                if n < SPLIT_LOADS:
-                    nc.sync.dma_start(out=raw[:, 0:F], in_=x[rows, 0, :])
-                    nc.sync.dma_start(out=raw[:, F:2 * F], in_=x[rows, 1, :])
-                else:
-                    nc.sync.dma_start(out=raw[:], in_=x[rows, :, :].rearrange("m c k -> m (c k)"))
+                nc.sync.dma_start(out=raw[:], in_=x[rows, :, :].rearrange("m c k -> m (c k)"))
             else:
-                cuts = 2 if n < SPLIT_LOADS else 1
+                cuts = 2 if n == 0 else 1
                 step = F // cuts
                 for h in range(cuts):
                     cols = slice(h * step, (h + 1) * step)
@@ -117,9 +101,6 @@ def tile_fftmlp_kernel(tc, x, filters_real, filters_imag, out):
             words = raws[n][:].bitcast(F32)
             stage = stage_pool.tile([P, 2 * F], BF16, name="stage", tag="stage", align_bytes=64)
             stage_words = stage[:].bitcast(F32)
-            wg = None
-            if kind == "W":
-                wg = wg_pool.tile([P, 2 * F], BF16, name="wg", tag="wg", align_bytes=64)
             for b in range(4):
                 tp = tp_pool.tile([P, 512], F32, name="tp", tag="tp")
                 if kind == "X":
@@ -133,49 +114,36 @@ def tile_fftmlp_kernel(tc, x, filters_real, filters_imag, out):
                     dst = stage_words[:, b * 512:(b + 1) * 512].rearrange("p (g m u) -> p g m u", g=2, u=2)
                 else:
                     dst = stage_words.rearrange("p (f c m u) -> p f c m u", f=2, c=4, u=2)[:, :, b, :, :]
-                if kind == "X" and b == 3:
-                    nc.vector.tensor_copy(out=dst, in_=src)
-                else:
-                    nc.scalar.copy(out=dst, in_=src)
-                if b % 2 == 0:
-                    continue
-                h = b // 2
-                if kind == "X":
+                nc.scalar.copy(out=dst, in_=src)
+            if kind == "X":
+                nc.vector.quantize_mx(out=x_codes[idx][:].bitcast(FP8X4), scales=x_scales[idx][:], in_=stage[:])
+            else:
+                wg = wg_pool.tile([P, 2 * F], BF16, name="wg", tag="wg", align_bytes=64)
+                nc.vector.tensor_tensor(out=wg[:, 0:F], in0=stage[:, 0:F], in1=stage[:, F:2 * F], op=ADD)
+                nc.vector.tensor_tensor(out=wg[:, F:2 * F], in0=stage[:, 0:F], in1=stage[:, F:2 * F], op=SUB)
+                cols = slice((idx % 2) * P, (idx % 2 + 1) * P)
+                for g in range(PASSES):
                     nc.vector.quantize_mx(
-                        out=x_codes[idx][:, h * 512:(h + 1) * 512].bitcast(FP8X4),
-                        scales=x_scales[idx][:, h * 512:(h + 1) * 512],
-                        in_=stage[:, h * F:(h + 1) * F],
+                        out=w_codes[idx // 2][:, g, cols].bitcast(FP8X4),
+                        scales=w_scales[idx // 2][:, g, cols],
+                        in_=wg[:, g * 512:(g + 1) * 512],
                     )
-                else:
-                    lo, hi = h * 1024, (h + 1) * 1024
-                    nc.vector.tensor_tensor(out=wg[:, lo:hi], in0=stage[:, lo:hi], in1=stage[:, F + lo:F + hi], op=ADD)
-                    nc.vector.tensor_tensor(out=wg[:, F + lo:F + hi], in0=stage[:, lo:hi], in1=stage[:, F + lo:F + hi], op=SUB)
-                    cols = slice((idx % 2) * P, (idx % 2 + 1) * P)
-                    for g in (2 * h, 2 * h + 1, 4 + 2 * h, 4 + 2 * h + 1):
-                        nc.vector.quantize_mx(
-                            out=w_codes[idx // 2][:, g, cols].bitcast(FP8X4),
-                            scales=w_scales[idx // 2][:, g, cols],
-                            in_=wg[:, g * 512:(g + 1) * 512],
-                        )
 
-        def multiply(i, ws):
-            width = len(ws) * P
-            j = ws[0] // 2
-            cols = slice((ws[0] % 2) * P, (ws[0] % 2) * P + width)
+        def multiply(i, j):
             acc = acc_pool.tile([P, 512], F32, name="acc", tag="acc")
             for g in range(PASSES):
                 nc.tensor.matmul_mx(
-                    out=acc[:, 0:width],
+                    out=acc[:, 0:NCOL],
                     lhsT=x_codes[i][:, g * P:(g + 1) * P].bitcast(FP8X4),
                     lhsT_scale=x_scales[i][:, g * P:(g + 1) * P],
-                    rhs=w_codes[j][:, g, cols].bitcast(FP8X4),
-                    rhs_scale=w_scales[j][:, g, cols],
+                    rhs=w_codes[j][:, g, :].bitcast(FP8X4),
+                    rhs_scale=w_scales[j][:, g, :],
                     start=(g == 0),
                     stop=(g == PASSES - 1),
                 )
-            res = res_pool.tile([P, PAIR], F32, name="res", tag="res")
-            nc.scalar.copy(out=res[:, 0:width], in_=acc[:, 0:width])
-            nc.sync.dma_start(out=out[i * P:(i + 1) * P, ws[0] * P:ws[0] * P + width], in_=res[:, 0:width])
+            res = res_pool.tile([P, NCOL], F32, name="res", tag="res")
+            nc.scalar.copy(out=res[:], in_=acc[:, 0:NCOL])
+            nc.sync.dma_start(out=out[i * P:(i + 1) * P, j * NCOL:(j + 1) * NCOL], in_=res[:])
 
         for n in range(RAW_BUFS):
             load(n)

@@ -25,9 +25,10 @@ LAG_W = 3
 LAG_X = 3
 RAW_BUFS = 6
 STAGE_BUFS = 8
-WARM_FIRST = 6
-WARM_EACH = 2
-WARM_UNITS = 6
+BLOCKS = (1, 1, 1, 1, 1, 1, 2, 2, 2, 2, 2)
+GROUPS_PER_UNIT = 1.5
+TP_BANKS = 5
+ACC_BANKS = 3
 
 
 def pe_sequence():
@@ -41,11 +42,16 @@ def pe_sequence():
             items.append((avail, j, i))
     items = sorted(items)
     seq = []
-    for n in range(len(UNITS)):
-        seq.append(("T", n, 0))
-        if items and items[0][0] <= n:
+    n = 0
+    for size in BLOCKS:
+        for k in range(size):
+            seq.append(("T", n, 0))
+            n += 1
+        budget = GROUPS_PER_UNIT * size
+        while budget > 0 and items and items[0][0] <= n - 1:
             seq.append(("M", items[0][2], items[0][1]))
             items = items[1:]
+            budget -= 1
     for it in items:
         seq.append(("M", it[2], it[1]))
     return seq
@@ -59,12 +65,10 @@ def tile_fftmlp_kernel(tc, x, filters_real, filters_imag, out):
         stage_pool = ctx.enter_context(tc.tile_pool(name="stagep", bufs=STAGE_BUFS))
         wg_pool = ctx.enter_context(tc.tile_pool(name="wgp", bufs=2))
         res_pool = ctx.enter_context(tc.tile_pool(name="resp", bufs=4))
-        tp_pool = ctx.enter_context(tc.psum_pool(name="tpp", bufs=4))
-        acc_pool = ctx.enter_context(tc.psum_pool(name="accp", bufs=4))
+        tp_pool = ctx.enter_context(tc.psum_pool(name="tpp", bufs=TP_BANKS))
+        acc_pool = ctx.enter_context(tc.psum_pool(name="accp", bufs=ACC_BANKS))
         ctx.enter_context(tc.manual_schedule())
 
-        warm = keep.tile([P, 512], BF16, name="warm")
-        nc.vector.memset(warm[:], 0.0)
         ident = keep.tile([P, P], F32, name="ident")
         make_identity(nc, ident[:])
 
@@ -89,12 +93,6 @@ def tile_fftmlp_kernel(tc, x, filters_real, filters_imag, out):
                     nc.sync.dma_start(out=raw[:, h * step:(h + 1) * step], in_=filters_real[rows, cols])
                     nc.sync.dma_start(out=raw[:, F + h * step:F + (h + 1) * step], in_=filters_imag[rows, cols])
             raws[n] = raw
-
-        warm_ps = acc_pool.tile([P, 512], F32, name="warm_ps", tag="acc")
-
-        def warm_up(count):
-            for d in range(count):
-                nc.tensor.matmul(out=warm_ps[:], lhsT=warm[:, 0:P], rhs=warm[:], start=True, stop=True)
 
         def transpose_unit(n):
             kind, idx = UNITS[n]
@@ -130,10 +128,10 @@ def tile_fftmlp_kernel(tc, x, filters_real, filters_imag, out):
                     )
 
         def multiply(i, j):
-            acc = acc_pool.tile([P, 512], F32, name="acc", tag="acc")
+            acc = acc_pool.tile([P, NCOL], F32, name="acc", tag="acc")
             for g in range(PASSES):
                 nc.tensor.matmul_mx(
-                    out=acc[:, 0:NCOL],
+                    out=acc[:],
                     lhsT=x_codes[i][:, g * P:(g + 1) * P].bitcast(FP8X4),
                     lhsT_scale=x_scales[i][:, g * P:(g + 1) * P],
                     rhs=w_codes[j][:, g, :].bitcast(FP8X4),
@@ -142,18 +140,15 @@ def tile_fftmlp_kernel(tc, x, filters_real, filters_imag, out):
                     stop=(g == PASSES - 1),
                 )
             res = res_pool.tile([P, NCOL], F32, name="res", tag="res")
-            nc.scalar.copy(out=res[:], in_=acc[:, 0:NCOL])
+            nc.scalar.copy(out=res[:], in_=acc[:])
             nc.sync.dma_start(out=out[i * P:(i + 1) * P, j * NCOL:(j + 1) * NCOL], in_=res[:])
 
         for n in range(RAW_BUFS):
             load(n)
         loaded = RAW_BUFS
-        warm_up(WARM_FIRST)
         for step in pe_sequence():
             if step[0] == "T":
                 transpose_unit(step[1])
-                if step[1] < WARM_UNITS:
-                    warm_up(WARM_EACH)
                 if loaded < len(UNITS):
                     load(loaded)
                     loaded += 1

from contextlib import ExitStack

import concourse.mybir as mybir
from concourse.masks import make_identity

F32 = mybir.dt.float32
BF16 = mybir.dt.bfloat16
U32 = mybir.dt.uint32
U8 = mybir.dt.uint8
FP8X4 = mybir.dt.float8_e4m3fn_x4
ADD = mybir.AluOpType.add
SUB = mybir.AluOpType.subtract

P = 128
B, F, O = 1024, 2048, 1024
FLOPS = 2 * B * O * 2 * F
PASSES = 8
NCOL = 256

UNITS = (
    ("W", 0), ("W", 1), ("X", 0), ("X", 1), ("X", 2), ("X", 3), ("W", 2), ("W", 3),
    ("X", 4), ("X", 5), ("X", 6), ("X", 7), ("W", 4), ("W", 5), ("W", 6), ("W", 7),
)
LAG_W = 3
LAG_X = 3
RAW_BUFS = 6
STAGE_BUFS = 8
BLOCKS = (1, 1, 1, 1, 1, 1, 2, 2, 2, 2, 2)
GROUPS_PER_UNIT = 1.5
TP_BANKS = 5
ACC_BANKS = 3


def pe_sequence():
    pos = {}
    for n, u in enumerate(UNITS):
        pos[u] = n
    items = []
    for j in range(O // NCOL):
        for i in range(B // P):
            avail = max(pos[("X", i)] + LAG_X, pos[("W", 2 * j)] + LAG_W, pos[("W", 2 * j + 1)] + LAG_W)
            items.append((avail, j, i))
    items = sorted(items)
    seq = []
    n = 0
    for size in BLOCKS:
        for k in range(size):
            seq.append(("T", n, 0))
            n += 1
        budget = GROUPS_PER_UNIT * size
        while budget > 0 and items and items[0][0] <= n - 1:
            seq.append(("M", items[0][2], items[0][1]))
            items = items[1:]
            budget -= 1
    for it in items:
        seq.append(("M", it[2], it[1]))
    return seq


def tile_fftmlp_kernel(tc, x, filters_real, filters_imag, out):
    nc = tc.nc
    with ExitStack() as ctx:
        keep = ctx.enter_context(tc.tile_pool(name="keep", bufs=1))
        raw_pool = ctx.enter_context(tc.tile_pool(name="rawp", bufs=RAW_BUFS))
        stage_pool = ctx.enter_context(tc.tile_pool(name="stagep", bufs=STAGE_BUFS))
        wg_pool = ctx.enter_context(tc.tile_pool(name="wgp", bufs=2))
        res_pool = ctx.enter_context(tc.tile_pool(name="resp", bufs=4))
        tp_pool = ctx.enter_context(tc.psum_pool(name="tpp", bufs=TP_BANKS))
        acc_pool = ctx.enter_context(tc.psum_pool(name="accp", bufs=ACC_BANKS))
        ctx.enter_context(tc.manual_schedule())

        ident = keep.tile([P, P], F32, name="ident")
        make_identity(nc, ident[:])

        x_codes = [keep.tile([P, PASSES * P], U32, name="xc%d" % i, align_bytes=64) for i in range(B // P)]
        x_scales = [keep.tile([P, PASSES * P], U8, name="xs%d" % i, align_bytes=64) for i in range(B // P)]
        w_codes = [keep.tile([P, PASSES, NCOL], U32, name="wc%d" % j, align_bytes=64) for j in range(O // NCOL)]
        w_scales = [keep.tile([P, PASSES, NCOL], U8, name="ws%d" % j, align_bytes=64) for j in range(O // NCOL)]

        raws = {}

        def load(n):
            kind, idx = UNITS[n]
            raw = raw_pool.tile([P, 2 * F], BF16, name="raw", tag="raw")
            rows = slice(idx * P, (idx + 1) * P)
            if kind == "X":
                nc.sync.dma_start(out=raw[:], in_=x[rows, :, :].rearrange("m c k -> m (c k)"))
            else:
                cuts = 2 if n == 0 else 1
                step = F // cuts
                for h in range(cuts):
                    cols = slice(h * step, (h + 1) * step)
                    nc.sync.dma_start(out=raw[:, h * step:(h + 1) * step], in_=filters_real[rows, cols])
                    nc.sync.dma_start(out=raw[:, F + h * step:F + (h + 1) * step], in_=filters_imag[rows, cols])
            raws[n] = raw

        def transpose_unit(n):
            kind, idx = UNITS[n]
            words = raws[n][:].bitcast(F32)
            stage = stage_pool.tile([P, 2 * F], BF16, name="stage", tag="stage", align_bytes=64)
            stage_words = stage[:].bitcast(F32)
            for b in range(4):
                tp = tp_pool.tile([P, 512], F32, name="tp", tag="tp")
                if kind == "X":
                    blocks = [4 * b, 4 * b + 1, 4 * b + 2, 4 * b + 3]
                else:
                    blocks = [2 * b, 2 * b + 1, 8 + 2 * b, 8 + 2 * b + 1]
                for s in range(4):
                    nc.tensor.transpose(tp[:, s * P:(s + 1) * P], words[:, blocks[s] * P:(blocks[s] + 1) * P], ident[:])
                src = tp[:].rearrange("p (g u m) -> p g m u", g=2, u=2)
                if kind == "X":
                    dst = stage_words[:, b * 512:(b + 1) * 512].rearrange("p (g m u) -> p g m u", g=2, u=2)
                else:
                    dst = stage_words.rearrange("p (f c m u) -> p f c m u", f=2, c=4, u=2)[:, :, b, :, :]
                nc.scalar.copy(out=dst, in_=src)
            if kind == "X":
                nc.vector.quantize_mx(out=x_codes[idx][:].bitcast(FP8X4), scales=x_scales[idx][:], in_=stage[:])
            else:
                wg = wg_pool.tile([P, 2 * F], BF16, name="wg", tag="wg", align_bytes=64)
                nc.vector.tensor_tensor(out=wg[:, 0:F], in0=stage[:, 0:F], in1=stage[:, F:2 * F], op=ADD)
                nc.vector.tensor_tensor(out=wg[:, F:2 * F], in0=stage[:, 0:F], in1=stage[:, F:2 * F], op=SUB)
                cols = slice((idx % 2) * P, (idx % 2 + 1) * P)
                for g in range(PASSES):
                    nc.vector.quantize_mx(
                        out=w_codes[idx // 2][:, g, cols].bitcast(FP8X4),
                        scales=w_scales[idx // 2][:, g, cols],
                        in_=wg[:, g * 512:(g + 1) * 512],
                    )

        def multiply(i, j):
            acc = acc_pool.tile([P, NCOL], F32, name="acc", tag="acc")
            for g in range(PASSES):
                nc.tensor.matmul_mx(
                    out=acc[:],
                    lhsT=x_codes[i][:, g * P:(g + 1) * P].bitcast(FP8X4),
                    lhsT_scale=x_scales[i][:, g * P:(g + 1) * P],
                    rhs=w_codes[j][:, g, :].bitcast(FP8X4),
                    rhs_scale=w_scales[j][:, g, :],
                    start=(g == 0),
                    stop=(g == PASSES - 1),
                )
            res = res_pool.tile([P, NCOL], F32, name="res", tag="res")
            nc.scalar.copy(out=res[:], in_=acc[:])
            nc.sync.dma_start(out=out[i * P:(i + 1) * P, j * NCOL:(j + 1) * NCOL], in_=res[:])

        for n in range(RAW_BUFS):
            load(n)
        loaded = RAW_BUFS
        for step in pe_sequence():
            if step[0] == "T":
                transpose_unit(step[1])
                if loaded < len(UNITS):
                    load(loaded)
                    loaded += 1
            else:
                multiply(step[1], step[2])
